import numpy as np
import ml_dtypes


def mxq(x, axis, fmt="e4m3"):
    dtype, down = {"e4m3": (ml_dtypes.float8_e4m3fn, 7), "e5m2": (ml_dtypes.float8_e5m2, 14)}[fmt]
    v = np.moveaxis(np.asarray(x, np.float32).astype(ml_dtypes.bfloat16).astype(np.float64), axis, -1)
    blocks = v.reshape(v.shape[:-1] + (-1, 32))
    amax = np.abs(blocks).max(-1, keepdims=True)
    byte = np.maximum(np.where(amax > 0, np.frexp(amax)[1] - 1 + 127, 0) - down, 1)
    scale = np.exp2(byte - 127.0)
    codes = (blocks / scale).astype(np.float32).astype(dtype).astype(np.float64)
    return np.moveaxis((codes * scale).reshape(v.shape), -1, axis)


WIDE = False


def mx_kscale(k):
    if not WIDE:
        return np.ones(k)
    levels = np.array([10, -10, 5, -5, 0])
    if k % 512:
        return np.exp2(np.random.permutation(np.resize(levels, k // 32))).repeat(32)
    a = np.empty((k // 512, 16))
    for p in range(k // 512):
        a[p, :8] = np.random.permutation(np.resize(levels, 8))
        for g in range(8):
            far = levels[np.abs(levels - a[p, g]) >= 10]
            a[p, g + 8] = far[np.random.randint(len(far))]
    return np.exp2(a.ravel()).repeat(32)


BF16 = ml_dtypes.bfloat16


def bf(x):
    return np.asarray(x, np.float32).astype(BF16)


def f64(x):
    return np.asarray(x).astype(np.float64)


B, D_IN, D_H = 512, 1024, 1024


def sigmoid(v):
    return 1.0 / (1.0 + np.exp(-v))


def setup_inputs():
    s, t = mx_kscale(D_IN), mx_kscale(D_H)

    def w_in():
        return bf(np.random.standard_normal((D_H, D_IN)) * 0.6 / np.sqrt(D_IN) / s[None, :])

    def w_rec():
        return bf(np.random.standard_normal((D_H, D_H)) * 0.6 / np.sqrt(D_H) / t[None, :])

    def bias():
        return bf(np.random.standard_normal(D_H) * 0.3)

    return {"incoming": bf(np.random.standard_normal((B, D_IN)) * s), "h": bf(np.random.standard_normal((B, D_H)) * t),
            "W_i": w_in(), "b_W_i": bias(), "W_c": w_in(), "b_W_c": bias(),
            "U_i": w_rec(), "b_U_i": bias(), "U_c": w_rec(), "b_U_c": bias()}


def core(incoming, h, W_i, b_W_i, W_c, b_W_c, U_i, b_U_i, U_c, b_U_c):
    xq = mxq(f64(incoming), 1, "e4m3")
    hq = mxq(f64(h), 1, "e4m3")
    I = sigmoid((xq @ mxq(f64(W_i), 1, "e4m3").T) + f64(b_W_i) + (hq @ mxq(f64(U_i), 1, "e4m3").T) + f64(b_U_i))
    C_head = (xq @ mxq(f64(W_c), 1, "e4m3").T) + f64(b_W_c) + (hq @ mxq(f64(U_c), 1, "e4m3").T) + f64(b_U_c)
    return I * C_head


def e4m3fn_bytes(y):
    return np.clip(np.asarray(y, np.float64), -448.0, 448.0).astype(np.float32).astype(ml_dtypes.float8_e4m3fn).view(np.uint8)


def reference(incoming, h, W_i, b_W_i, W_c, b_W_c, U_i, b_U_i, U_c, b_U_c):
    out = core(incoming, h, W_i, b_W_i, W_c, b_W_c, U_i, b_U_i, U_c, b_U_c)
    s = np.max(np.abs(out), axis=-1, keepdims=True) / 448.0
    return out, e4m3fn_bytes(out / s)

@@ -1,0 +1,276 @@
+from contextlib import ExitStack
+
+import concourse.mybir as mybir
+from concourse.masks import make_identity
+
+F32 = mybir.dt.float32
+BF16 = mybir.dt.bfloat16
+U32 = mybir.dt.uint32
+U8 = mybir.dt.uint8
+FP8X4 = mybir.dt.float8_e4m3fn_x4
+FP8 = mybir.dt.float8_e4m3fn
+ALU = mybir.AluOpType
+ACT = mybir.ActivationFunctionType
+AX = mybir.AxisListType
+
+FLOPS = 2 * 512 * 1024 * 1024 * 4
+
+P = 128
+V_COPY_UNTIL = 24
+V_COPY_EVERY = 4
+GP_HELPS = True
+S_CAST_COLS = 384
+
+
+def tile_lstmcell_pa_kernel(tc, incoming, h, W_i, b_W_i, W_c, b_W_c, U_i, b_U_i, U_c, b_U_c, out_0, out_1):
+    nc = tc.nc
+    units = [(incoming, 0), (h, 0), (W_i, 0), (U_i, 0), (W_c, 0), (U_c, 0), (W_i, 512), (U_i, 512), (W_c, 512), (U_c, 512)]
+    weight_units = {("i", 0): (2, 3), ("c", 0): (4, 5), ("i", 1): (6, 7), ("c", 1): (8, 9)}
+
+    with ExitStack() as ctx:
+        const = ctx.enter_context(tc.tile_pool(name="const", bufs=1))
+        rawp = ctx.enter_context(tc.tile_pool(name="rawp", bufs=1))
+        keep = ctx.enter_context(tc.tile_pool(name="keep", bufs=1))
+        grpp = ctx.enter_context(tc.tile_pool(name="grpp", bufs=6))
+        work = ctx.enter_context(tc.tile_pool(name="work", bufs=3))
+        sigp = ctx.enter_context(tc.tile_pool(name="sigp", bufs=6))
+        tpp = ctx.enter_context(tc.psum_pool(name="tpp", bufs=4))
+        accp = ctx.enter_context(tc.psum_pool(name="accp", bufs=4))
+        ctx.enter_context(tc.manual_schedule())
+
+        brow = const.tile([P, 2048], BF16, name="brow")
+        ones = const.tile([P, P], BF16, name="ones")
+        zeros = const.tile([P, 1], F32, name="zeros")
+        warm = const.tile([P, 1], F32, name="warm")
+        ident = const.tile([P, P], F32, name="ident")
+        bias = const.tile([P, 2048], F32, name="bias")
+        stat = const.tile([P, 12], F32, name="stat")
+        pm = const.tile([P, 1], F32, name="pm")
+        qs = const.tile([P, 4], F32, name="qs")
+        rq = const.tile([P, 4], F32, name="rq")
+        nc.vector.memset(zeros[:], 0.0)
+        nc.vector.memset(brow[:], 0.0)
+        nc.vector.memset(ones[:], 1.0)
+        make_identity(nc, ident[:])
+        nc.scalar.dma_start(out=brow[0:1, 0:1024], in_=b_W_i.rearrange("(o n) -> o n", o=1))
+        nc.scalar.dma_start(out=brow[1:2, 0:1024], in_=b_U_i.rearrange("(o n) -> o n", o=1))
+        nc.scalar.dma_start(out=brow[0:1, 1024:2048], in_=b_W_c.rearrange("(o n) -> o n", o=1))
+        nc.scalar.dma_start(out=brow[1:2, 1024:2048], in_=b_U_c.rearrange("(o n) -> o n", o=1))
+        nc.scalar.activation(out=warm[:], in_=zeros[:], func=ACT.Sigmoid)
+
+        raw = {}
+        for u in range(10):
+            src, r0 = units[u]
+            for pair in range(2):
+                rows_in = src[r0 + pair * 256 : r0 + (pair + 1) * 256, :].rearrange("(p j) k -> p j k", j=2)
+                if u == 0 and pair == 0:
+                    for g in range(2):
+                        t = rawp.tile([P, 2, 512], BF16, name="rawfirst%d" % g)
+                        nc.sync.dma_start(out=t[:], in_=rows_in[:, :, g * 512 : (g + 1) * 512])
+                        raw[4 * u + 2 * pair + g] = (t, 0)
+                else:
+                    t = rawp.tile([P, 2, 1024], BF16, name="raw%d_%d" % (u, pair))
+                    nc.sync.dma_start(out=t[:], in_=rows_in)
+                    for g in range(2):
+                        raw[4 * u + 2 * pair + g] = (t, 256 * g)
+
+        codes = {}
+        scales = {}
+        for u in range(10):
+            for g in range(2):
+                codes[(u, g)] = keep.tile([P, 512], U32, name="codes%d_%d" % (u, g), align_bytes=64)
+                scales[(u, g)] = keep.tile([P, 512], U8, name="scales%d_%d" % (u, g), align_bytes=64)
+        res = [keep.tile([P, 1024], F32, name="res%d" % m) for m in range(4)]
+        res8 = [keep.tile([P, 1024], FP8, name="resb%d" % m) for m in range(4)]
+
+        tps = {}
+        grps = {}
+        accs = {}
+        sigs = {}
+        cands = {}
+        pending = []
+        later = []
+        head = [0]
+
+        def transposes(b):
+            words = raw[b][0][:].bitcast(F32)
+            w0 = raw[b][1]
+            tp = tpp.tile([P, 512], F32, name="tp")
+            for j in range(2):
+                for e in range(2):
+                    nc.tensor.transpose(tp[:, (2 * j + e) * P : (2 * j + e + 1) * P], words[:, j, w0 + e : w0 + 256 : 2], ident[:])
+            tps[b] = tp
+
+        def copy_out(b):
+            grp = grpp.tile([P, 1024], BF16, name="grp", align_bytes=64)
+            dst = grp[:].bitcast(F32).rearrange("p (j r e) -> p j r e", j=2, e=2)
+            srcv = tps[b][:].rearrange("p (j e r) -> p j r e", j=2, e=2)
+            if b < V_COPY_UNTIL and b % V_COPY_EVERY == V_COPY_EVERY - 1:
+                nc.vector.tensor_copy(out=dst, in_=srcv)
+            else:
+                nc.scalar.copy(out=dst, in_=srcv)
+            grps[b] = grp
+
+        def quantize(b):
+            u, pair, g = b // 4, (b % 4) // 2, b % 2
+            cols = slice(pair * 256, (pair + 1) * 256)
+            nc.vector.quantize_mx(out=codes[(u, g)][:, cols].bitcast(FP8X4), scales=scales[(u, g)][:, cols], in_=grps[b][:])
+
+        def flush_quant():
+            for b in pending:
+                quantize(b)
+            pending.clear()
+
+        def pop_later(n_big):
+            done = 0
+            while head[0] < len(later) and done < n_big:
+                big, fn = later[head[0]]
+                head[0] += 1
+                fn()
+                if big:
+                    done += 1
+
+        def step_t(b):
+            transposes(b)
+            copy_out(b)
+            flush_quant()
+            pending.append(b)
+            pop_later(1)
+
+        def bias_rows():
+            for q in range(4):
+                bp = tpp.tile([P, 512], F32, name="tp")
+                nc.tensor.matmul(out=bp[:], lhsT=ones[:], rhs=brow[:, q * 512 : (q + 1) * 512], start=True, stop=True)
+                nc.vector.tensor_copy(out=bias[:, q * 512 : (q + 1) * 512], in_=bp[:])
+
+        def group(gate, nh, m, c0=0, width=512):
+            acc = accp.tile([P, width], F32, name="acc")
+            rows = slice(m * P, (m + 1) * P)
+            n = 0
+            for a_unit, w_unit in zip((0, 1), weight_units[(gate, nh)]):
+                for g in range(2):
+                    nc.tensor.matmul_mx(
+                        out=acc[:],
+                        lhsT=codes[(a_unit, g)][:, rows].bitcast(FP8X4),
+                        lhsT_scale=scales[(a_unit, g)][:, rows],
+                        rhs=codes[(w_unit, g)][:, c0 : c0 + width].bitcast(FP8X4),
+                        rhs_scale=scales[(w_unit, g)][:, c0 : c0 + width],
+                        start=(n == 0),
+                        stop=(n == 3),
+                    )
+                    n += 1
+            return acc
+
+        def add_bias(dst, acc_ap, bias_ap):
+            nc.vector.tensor_tensor(
+                out=dst.rearrange("p (b r j) -> p b r j", r=P, j=2),
+                in0=acc_ap.rearrange("p (b j r) -> p b r j", r=P, j=2),
+                in1=bias_ap.rearrange("p (b r j) -> p b r j", r=P, j=2),
+                op=ALU.add,
+            )
+
+        def out_rows(m):
+            return slice((m // 2) * 256 + m % 2, (m // 2 + 1) * 256, 2)
+
+        def step_i(nh, m):
+            flush_quant()
+            acc = group("i", nh, m)
+            pre = work.tile([P, 512], F32, name="pre")
+            add_bias(pre[:], acc[:], bias[:, nh * 512 : (nh + 1) * 512])
+            sig = sigp.tile([P, 512], F32, name="sig")
+            nc.scalar.activation(out=sig[:], in_=pre[:], func=ACT.Sigmoid)
+            sigs[(nh, m)] = sig
+            pop_later(1)
+
+        def store_bytes(m):
+            nc.sync.dma_start(out=out_1[out_rows(m), :], in_=res8[m][:].bitcast(U8))
+
+        def add_c(nh, m, c0=0, width=512):
+            acc = group("c", nh, m, c0, width)
+            if c0 == 0:
+                cands[(nh, m)] = work.tile([P, 512], F32, name="cand")
+            b0 = 1024 + nh * 512 + c0
+            add_bias(cands[(nh, m)][:, c0 : c0 + width], acc[:], bias[:, b0 : b0 + width])
+
+        def mult(eng, nh, m, c0=0, width=512):
+            o0 = nh * 512 + c0
+            eng.tensor_tensor(out=res[m][:, o0 : o0 + width], in0=sigs[(nh, m)][:, c0 : c0 + width], in1=cands[(nh, m)][:, c0 : c0 + width], op=ALU.mult)
+
+        def store_half(nh, m):
+            cols = slice(nh * 512, (nh + 1) * 512)
+            nc.sync.dma_start(out=out_0[out_rows(m), cols], in_=res[m][:, cols])
+
+        def amax(m, slot, o0, width):
+            nc.vector.tensor_reduce(out=stat[:, 3 * m + slot : 3 * m + slot + 1], in_=res[m][:, o0 : o0 + width], axis=AX.X, op=ALU.max, apply_absolute_value=True)
+
+        def qscale(m):
+            nc.vector.tensor_scalar(out=qs[:, m : m + 1], in0=stat[:, 3 * m : 3 * m + 1], scalar1=stat[:, 3 * m + 1 : 3 * m + 2], scalar2=1.0 / 448.0, op0=ALU.max, op1=ALU.mult)
+
+        def recip(m):
+            nc.vector.reciprocal(out=rq[:, m : m + 1], in_=qs[:, m : m + 1])
+
+        def cast_s(m, a, z):
+            nc.scalar.activation(out=res8[m][:, a:z], in_=res[m][:, a:z], func=ACT.Identity, scale=rq[:, m : m + 1], bias=zeros[:, 0:1], saturate=False)
+
+        def cast_v(m, a, z):
+            nc.vector.tensor_scalar(out=res8[m][:, a:z], in0=res[m][:, a:z], scalar1=rq[:, m : m + 1], scalar2=None, op0=ALU.mult, saturate=False)
+
+        def step_c0(m):
+            flush_quant()
+            add_c(0, m)
+            pop_later(1)
+
+            def mult_store():
+                mult(nc.vector, 0, m)
+                store_half(0, m)
+
+            later.append((True, mult_store))
+            later.append((True, lambda: amax(m, 0, 0, 512)))
+
+        for b in range(24):
+            step_t(b)
+            if b == 7:
+                bias_rows()
+        for m in range(4):
+            step_i(0, m)
+            step_c0(m)
+            for b in range(24 + 4 * m, 28 + 4 * m):
+                step_t(b)
+        helper = nc.gpsimd if GP_HELPS else nc.vector
+        for m in range(3):
+            step_i(1, m)
+            if m == 2:
+                qscale(0)
+            add_c(1, m)
+            mult(helper, 1, m)
+            store_half(1, m)
+            if m == 2:
+                recip(0)
+                cast_s(0, 0, 1024)
+                store_bytes(0)
+            if m >= 1:
+                amax(m - 1, 1, 512, 512)
+        m = 3
+        step_i(1, m)
+        qscale(1)
+        add_c(1, m, 0, 256)
+        recip(1)
+        cast_s(1, 0, 1024)
+        store_bytes(1)
+        amax(2, 1, 512, 512)
+        mult(helper, 1, m, 0, 256)
+        add_c(1, m, 256, 256)
+        qscale(2)
+        amax(m, 1, 512, 256)
+        recip(2)
+        cast_s(2, 0, 1024)
+        store_bytes(2)
+        mult(nc.vector, 1, m, 256, 256)
+        store_half(1, m)
+        nc.vector.tensor_scalar(out=pm[:], in0=stat[:, 3 * m : 3 * m + 1], scalar1=stat[:, 3 * m + 1 : 3 * m + 2], scalar2=1.0 / 448.0, op0=ALU.max, op1=ALU.mult)
+        amax(m, 2, 768, 256)
+        nc.vector.tensor_scalar(out=qs[:, m : m + 1], in0=stat[:, 3 * m + 2 : 3 * m + 3], scalar1=1.0 / 448.0, scalar2=pm[:, 0:1], op0=ALU.mult, op1=ALU.max)
+        recip(m)
+        cast_s(m, 0, S_CAST_COLS)
+        cast_v(m, S_CAST_COLS, 1024)
+        store_bytes(m)

@@ -16,9 +16,8 @@ AX = mybir.AxisListType
 FLOPS = 2 * 512 * 1024 * 1024 * 4
 
 P = 128
-V_COPY_UNTIL = 24
+V_COPY_UNTIL = 40
 V_COPY_EVERY = 4
-GP_HELPS = True
 S_CAST_COLS = 384
 
 
@@ -34,8 +33,7 @@ def tile_lstmcell_pa_kernel(tc, incoming, h, W_i, b_W_i, W_c, b_W_c, U_i, b_U_i,
         grpp = ctx.enter_context(tc.tile_pool(name="grpp", bufs=6))
         work = ctx.enter_context(tc.tile_pool(name="work", bufs=3))
         sigp = ctx.enter_context(tc.tile_pool(name="sigp", bufs=6))
-        tpp = ctx.enter_context(tc.psum_pool(name="tpp", bufs=4))
-        accp = ctx.enter_context(tc.psum_pool(name="accp", bufs=4))
+        psum = ctx.enter_context(tc.psum_pool(name="psum", bufs=8))
         ctx.enter_context(tc.manual_schedule())
 
         brow = const.tile([P, 2048], BF16, name="brow")
@@ -95,7 +93,7 @@ def tile_lstmcell_pa_kernel(tc, incoming, h, W_i, b_W_i, W_c, b_W_c, U_i, b_U_i,
         def transposes(b):
             words = raw[b][0][:].bitcast(F32)
             w0 = raw[b][1]
-            tp = tpp.tile([P, 512], F32, name="tp")
+            tp = psum.tile([P, 512], F32, name="bank")
             for j in range(2):
                 for e in range(2):
                     nc.tensor.transpose(tp[:, (2 * j + e) * P : (2 * j + e + 1) * P], words[:, j, w0 + e : w0 + 256 : 2], ident[:])
@@ -139,12 +137,12 @@ def tile_lstmcell_pa_kernel(tc, incoming, h, W_i, b_W_i, W_c, b_W_c, U_i, b_U_i,
 
         def bias_rows():
             for q in range(4):
-                bp = tpp.tile([P, 512], F32, name="tp")
+                bp = psum.tile([P, 512], F32, name="bank")
                 nc.tensor.matmul(out=bp[:], lhsT=ones[:], rhs=brow[:, q * 512 : (q + 1) * 512], start=True, stop=True)
-                nc.vector.tensor_copy(out=bias[:, q * 512 : (q + 1) * 512], in_=bp[:])
+                nc.scalar.copy(out=bias[:, q * 512 : (q + 1) * 512], in_=bp[:])
 
         def group(gate, nh, m, c0=0, width=512):
-            acc = accp.tile([P, width], F32, name="acc")
+            acc = psum.tile([P, width], F32, name="bank")
             rows = slice(m * P, (m + 1) * P)
             n = 0
             for a_unit, w_unit in zip((0, 1), weight_units[(gate, nh)]):
@@ -215,60 +213,49 @@ def tile_lstmcell_pa_kernel(tc, incoming, h, W_i, b_W_i, W_c, b_W_c, U_i, b_U_i,
         def cast_v(m, a, z):
             nc.vector.tensor_scalar(out=res8[m][:, a:z], in0=res[m][:, a:z], scalar1=rq[:, m : m + 1], scalar2=None, op0=ALU.mult, saturate=False)
 
-        def step_c0(m):
-            flush_quant()
-            add_c(0, m)
-            pop_later(1)
-
-            def mult_store():
-                mult(nc.vector, 0, m)
-                store_half(0, m)
-
-            later.append((True, mult_store))
-            later.append((True, lambda: amax(m, 0, 0, 512)))
-
-        for b in range(24):
+        for b in range(40):
             step_t(b)
             if b == 7:
                 bias_rows()
-        for m in range(4):
-            step_i(0, m)
-            step_c0(m)
-            for b in range(24 + 4 * m, 28 + 4 * m):
-                step_t(b)
-        helper = nc.gpsimd if GP_HELPS else nc.vector
+        flush_quant()
         for m in range(3):
-            step_i(1, m)
-            if m == 2:
-                qscale(0)
-            add_c(1, m)
-            mult(helper, 1, m)
-            store_half(1, m)
-            if m == 2:
-                recip(0)
-                cast_s(0, 0, 1024)
-                store_bytes(0)
+            step_i(0, m)
+            add_c(0, m)
+            mult(nc.gpsimd, 0, m)
+            store_half(0, m)
             if m >= 1:
                 amax(m - 1, 1, 512, 512)
+            step_i(1, m)
+            if m >= 1:
+                qscale(m - 1)
+            add_c(1, m)
+            mult(nc.gpsimd, 1, m)
+            store_half(1, m)
+            if m >= 1:
+                recip(m - 1)
+                cast_s(m - 1, 0, 1024)
+                store_bytes(m - 1)
+            amax(m, 0, 0, 512)
         m = 3
-        step_i(1, m)
-        qscale(1)
-        add_c(1, m, 0, 256)
-        recip(1)
-        cast_s(1, 0, 1024)
-        store_bytes(1)
+        step_i(0, m)
+        add_c(0, m)
+        mult(nc.gpsimd, 0, m)
+        store_half(0, m)
         amax(2, 1, 512, 512)
-        mult(helper, 1, m, 0, 256)
-        add_c(1, m, 256, 256)
+        step_i(1, m)
         qscale(2)
-        amax(m, 1, 512, 256)
+        add_c(1, m, 0, 256)
         recip(2)
         cast_s(2, 0, 1024)
         store_bytes(2)
+        amax(m, 0, 0, 512)
+        add_c(1, m, 256, 256)
+        mult(nc.vector, 1, m, 0, 256)
         mult(nc.vector, 1, m, 256, 256)
         store_half(1, m)
-        nc.vector.tensor_scalar(out=pm[:], in0=stat[:, 3 * m : 3 * m + 1], scalar1=stat[:, 3 * m + 1 : 3 * m + 2], scalar2=1.0 / 448.0, op0=ALU.max, op1=ALU.mult)
+        amax(m, 1, 512, 256)
         amax(m, 2, 768, 256)
+        nc.vector.tensor_scalar(out=pm[:], in0=stat[:, 3 * m : 3 * m + 1], scalar1=stat[:, 3 * m + 1 : 3 * m + 2], scalar2=1.0 / 448.0, op0=ALU.max, op1=ALU.mult)
         nc.vector.tensor_scalar(out=qs[:, m : m + 1], in0=stat[:, 3 * m + 2 : 3 * m + 3], scalar1=1.0 / 448.0, scalar2=pm[:, 0:1], op0=ALU.mult, op1=ALU.max)
         recip(m)
         cast_s(m, 0, S_CAST_COLS)

@@ -19,6 +19,7 @@ P = 128
 V_COPY_UNTIL = 40
 V_COPY_EVERY = 4
 S_CAST_COLS = 384
+FIRST_RUN = 24
 
 
 def tile_lstmcell_pa_kernel(tc, incoming, h, W_i, b_W_i, W_c, b_W_c, U_i, b_U_i, U_c, b_U_c, out_0, out_1):
@@ -33,6 +34,7 @@ def tile_lstmcell_pa_kernel(tc, incoming, h, W_i, b_W_i, W_c, b_W_c, U_i, b_U_i,
         grpp = ctx.enter_context(tc.tile_pool(name="grpp", bufs=6))
         work = ctx.enter_context(tc.tile_pool(name="work", bufs=3))
         sigp = ctx.enter_context(tc.tile_pool(name="sigp", bufs=6))
+        rop = ctx.enter_context(tc.tile_pool(name="rop", bufs=1))
         psum = ctx.enter_context(tc.psum_pool(name="psum", bufs=8))
         ctx.enter_context(tc.manual_schedule())
 
@@ -213,45 +215,136 @@ def tile_lstmcell_pa_kernel(tc, incoming, h, W_i, b_W_i, W_c, b_W_c, U_i, b_U_i,
         def cast_v(m, a, z):
             nc.vector.tensor_scalar(out=res8[m][:, a:z], in0=res[m][:, a:z], scalar1=rq[:, m : m + 1], scalar2=None, op0=ALU.mult, saturate=False)
 
-        for b in range(40):
-            step_t(b)
+        ro = {}
+        pres = {}
+
+        def reorder(eng_is_vector, b):
+            words = raw[b][0][:].bitcast(F32)
+            w0 = raw[b][1]
+            t = rop.tile([P, 512], F32, name="ro%d" % b)
+            dst = t[:].rearrange("p (j e q) -> p j e q", j=2, e=2)
+            srcv = words[:, :, w0 : w0 + 256].rearrange("p j (q e) -> p j e q", e=2)
+            if eng_is_vector:
+                nc.vector.tensor_copy(out=dst, in_=srcv)
+            else:
+                nc.scalar.copy(out=dst, in_=srcv)
+            ro[b] = t
+
+        def transposes_contig(b):
+            tp = psum.tile([P, 512], F32, name="bank")
+            for q in range(4):
+                nc.tensor.transpose(tp[:, q * P : (q + 1) * P], ro[b][:, q * P : (q + 1) * P], ident[:])
+            tps[b] = tp
+
+        def gate_mm(nh, m):
+            accs[("i", nh, m)] = group("i", nh, m)
+
+        def gate_add(nh, m):
+            pre = work.tile([P, 512], F32, name="pre")
+            add_bias(pre[:], accs[("i", nh, m)][:], bias[:, nh * 512 : (nh + 1) * 512])
+            pres[(nh, m)] = pre
+
+        def gate_sig(nh, m):
+            sig = sigp.tile([P, 512], F32, name="sig")
+            nc.scalar.activation(out=sig[:], in_=pres[(nh, m)][:], func=ACT.Sigmoid)
+            sigs[(nh, m)] = sig
+
+        for b in range(FIRST_RUN):
+            transposes(b)
+            copy_out(b)
+            if b >= 1:
+                quantize(b - 1)
             if b == 7:
                 bias_rows()
-        flush_quant()
-        for m in range(3):
-            step_i(0, m)
-            add_c(0, m)
-            mult(nc.gpsimd, 0, m)
-            store_half(0, m)
-            if m >= 1:
-                amax(m - 1, 1, 512, 512)
-            step_i(1, m)
-            if m >= 1:
-                qscale(m - 1)
-            add_c(1, m)
-            mult(nc.gpsimd, 1, m)
-            store_half(1, m)
-            if m >= 1:
-                recip(m - 1)
-                cast_s(m - 1, 0, 1024)
-                store_bytes(m - 1)
-            amax(m, 0, 0, 512)
+        quantize(FIRST_RUN - 1)
+
+        gate_mm(0, 0)
+        for b in range(24, 28):
+            reorder(True, b)
+        gate_add(0, 0)
+        reorder(False, 28)
+        reorder(False, 29)
+        gate_sig(0, 0)
+        add_c(0, 0)
+        mult(nc.gpsimd, 0, 0)
+        store_half(0, 0)
+        for b in range(30, 34):
+            reorder(False, b)
+        gate_mm(0, 1)
+        gate_add(0, 1)
+        gate_sig(0, 1)
+        add_c(0, 1)
+        mult(nc.gpsimd, 0, 1)
+        store_half(0, 1)
+        amax(0, 0, 0, 512)
+        for b in range(34, 38):
+            reorder(False, b)
+        gate_mm(0, 2)
+        gate_add(0, 2)
+        gate_sig(0, 2)
+        add_c(0, 2)
+        mult(nc.gpsimd, 0, 2)
+        store_half(0, 2)
+        amax(1, 0, 0, 512)
+        reorder(False, 38)
+        reorder(False, 39)
+        gate_mm(0, 3)
+        gate_add(0, 3)
+        add_c(0, 3)
+
+        for b in range(FIRST_RUN, 40):
+            transposes_contig(b)
+            copy_out(b)
+            if b > FIRST_RUN:
+                quantize(b - 1)
+        quantize(39)
+
+        gate_sig(0, 3)
+        mult(nc.gpsimd, 0, 3)
+        store_half(0, 3)
+        gate_mm(1, 0)
+        gate_mm(1, 1)
+        gate_add(1, 0)
+        gate_sig(1, 0)
+        gate_add(1, 1)
+        gate_sig(1, 1)
+        add_c(1, 0)
+        mult(nc.gpsimd, 1, 0)
+        store_half(1, 0)
+        amax(2, 0, 0, 512)
+        add_c(1, 1)
+        mult(nc.gpsimd, 1, 1)
+        store_half(1, 1)
+        amax(3, 0, 0, 512)
+        gate_mm(1, 2)
+        gate_add(1, 2)
+        gate_sig(1, 2)
+        amax(0, 1, 512, 512)
+        add_c(1, 2)
+        mult(nc.gpsimd, 1, 2)
+        store_half(1, 2)
+        qscale(0)
+        amax(1, 1, 512, 512)
+        recip(0)
+        cast_s(0, 0, 1024)
+        store_bytes(0)
         m = 3
-        step_i(0, m)
-        add_c(0, m)
-        mult(nc.gpsimd, 0, m)
-        store_half(0, m)
-        amax(2, 1, 512, 512)
-        step_i(1, m)
-        qscale(2)
+        gate_mm(1, m)
+        gate_add(1, m)
+        gate_sig(1, m)
+        qscale(1)
         add_c(1, m, 0, 256)
+        recip(1)
+        cast_s(1, 0, 1024)
+        store_bytes(1)
+        amax(2, 1, 512, 512)
+        add_c(1, m, 256, 256)
+        qscale(2)
+        mult(nc.vector, 1, m, 0, 256)
         recip(2)
+        mult(nc.vector, 1, m, 256, 256)
         cast_s(2, 0, 1024)
         store_bytes(2)
-        amax(m, 0, 0, 512)
-        add_c(1, m, 256, 256)
-        mult(nc.vector, 1, m, 0, 256)
-        mult(nc.vector, 1, m, 256, 256)
         store_half(1, m)
         amax(m, 1, 512, 256)
         amax(m, 2, 768, 256)

@@ -19,7 +19,7 @@ P = 128
 V_COPY_UNTIL = 40
 V_COPY_EVERY = 4
 S_CAST_COLS = 384
-FIRST_RUN = 24
+FIRST_RUN = 32
 
 
 def tile_lstmcell_pa_kernel(tc, incoming, h, W_i, b_W_i, W_c, b_W_c, U_i, b_U_i, U_c, b_U_c, out_0, out_1):
@@ -259,17 +259,15 @@ def tile_lstmcell_pa_kernel(tc, incoming, h, W_i, b_W_i, W_c, b_W_c, U_i, b_U_i,
         quantize(FIRST_RUN - 1)
 
         gate_mm(0, 0)
-        for b in range(24, 28):
-            reorder(True, b)
+        for b in range(32, 36):
+            reorder(False, b)
         gate_add(0, 0)
-        reorder(False, 28)
-        reorder(False, 29)
         gate_sig(0, 0)
         add_c(0, 0)
         mult(nc.gpsimd, 0, 0)
         store_half(0, 0)
-        for b in range(30, 34):
-            reorder(False, b)
+        reorder(False, 36)
+        reorder(False, 37)
         gate_mm(0, 1)
         gate_add(0, 1)
         gate_sig(0, 1)
@@ -277,8 +275,8 @@ def tile_lstmcell_pa_kernel(tc, incoming, h, W_i, b_W_i, W_c, b_W_c, U_i, b_U_i,
         mult(nc.gpsimd, 0, 1)
         store_half(0, 1)
         amax(0, 0, 0, 512)
-        for b in range(34, 38):
-            reorder(False, b)
+        reorder(False, 38)
+        reorder(False, 39)
         gate_mm(0, 2)
         gate_add(0, 2)
         gate_sig(0, 2)
@@ -286,11 +284,10 @@ def tile_lstmcell_pa_kernel(tc, incoming, h, W_i, b_W_i, W_c, b_W_c, U_i, b_U_i,
         mult(nc.gpsimd, 0, 2)
         store_half(0, 2)
         amax(1, 0, 0, 512)
-        reorder(False, 38)
-        reorder(False, 39)
         gate_mm(0, 3)
         gate_add(0, 3)
         add_c(0, 3)
+        amax(2, 0, 0, 512)
 
         for b in range(FIRST_RUN, 40):
             transposes_contig(b)
@@ -311,7 +308,6 @@ def tile_lstmcell_pa_kernel(tc, incoming, h, W_i, b_W_i, W_c, b_W_c, U_i, b_U_i,
         add_c(1, 0)
         mult(nc.gpsimd, 1, 0)
         store_half(1, 0)
-        amax(2, 0, 0, 512)
         add_c(1, 1)
         mult(nc.gpsimd, 1, 1)
         store_half(1, 1)

@@ -249,54 +249,52 @@ def tile_lstmcell_pa_kernel(tc, incoming, h, W_i, b_W_i, W_c, b_W_c, U_i, b_U_i,
             nc.scalar.activation(out=sig[:], in_=pres[(nh, m)][:], func=ACT.Sigmoid)
             sigs[(nh, m)] = sig
 
-        for b in range(FIRST_RUN):
+        for b in range(32):
             transposes(b)
             copy_out(b)
             if b >= 1:
                 quantize(b - 1)
             if b == 7:
                 bias_rows()
-        quantize(FIRST_RUN - 1)
-
+        quantize(32 - 1)
         gate_mm(0, 0)
-        for b in range(32, 36):
-            reorder(False, b)
+        reorder(False, 32)
+        reorder(False, 33)
+        reorder(False, 34)
+        reorder(False, 35)
         gate_add(0, 0)
         gate_sig(0, 0)
         add_c(0, 0)
         mult(nc.gpsimd, 0, 0)
         store_half(0, 0)
+        gate_mm(0, 1)
         reorder(False, 36)
         reorder(False, 37)
-        gate_mm(0, 1)
         gate_add(0, 1)
         gate_sig(0, 1)
         add_c(0, 1)
         mult(nc.gpsimd, 0, 1)
         store_half(0, 1)
         amax(0, 0, 0, 512)
+        gate_mm(0, 2)
         reorder(False, 38)
         reorder(False, 39)
-        gate_mm(0, 2)
         gate_add(0, 2)
-        gate_sig(0, 2)
         add_c(0, 2)
-        mult(nc.gpsimd, 0, 2)
-        store_half(0, 2)
         amax(1, 0, 0, 512)
-        gate_mm(0, 3)
-        gate_add(0, 3)
-        add_c(0, 3)
-        amax(2, 0, 0, 512)
-
-        for b in range(FIRST_RUN, 40):
+        for b in range(32, 40):
             transposes_contig(b)
             copy_out(b)
-            if b > FIRST_RUN:
+            if b > 32:
                 quantize(b - 1)
         quantize(39)
-
+        gate_sig(0, 2)
+        mult(nc.gpsimd, 0, 2)
+        store_half(0, 2)
+        gate_mm(0, 3)
+        gate_add(0, 3)
         gate_sig(0, 3)
+        add_c(0, 3)
         mult(nc.gpsimd, 0, 3)
         store_half(0, 3)
         gate_mm(1, 0)
@@ -308,6 +306,7 @@ def tile_lstmcell_pa_kernel(tc, incoming, h, W_i, b_W_i, W_c, b_W_c, U_i, b_U_i,
         add_c(1, 0)
         mult(nc.gpsimd, 1, 0)
         store_half(1, 0)
+        amax(2, 0, 0, 512)
         add_c(1, 1)
         mult(nc.gpsimd, 1, 1)
         store_half(1, 1)

from contextlib import ExitStack

import concourse.mybir as mybir
from concourse.masks import make_identity

F32 = mybir.dt.float32
BF16 = mybir.dt.bfloat16
U32 = mybir.dt.uint32
U8 = mybir.dt.uint8
FP8X4 = mybir.dt.float8_e4m3fn_x4
FP8 = mybir.dt.float8_e4m3fn
ALU = mybir.AluOpType
ACT = mybir.ActivationFunctionType
AX = mybir.AxisListType

FLOPS = 2 * 512 * 1024 * 1024 * 4

P = 128
V_COPY_UNTIL = 40
V_COPY_EVERY = 4
S_CAST_COLS = 384
FIRST_RUN = 32


def tile_lstmcell_pa_kernel(tc, incoming, h, W_i, b_W_i, W_c, b_W_c, U_i, b_U_i, U_c, b_U_c, out_0, out_1):
    nc = tc.nc
    units = [(incoming, 0), (h, 0), (W_i, 0), (U_i, 0), (W_c, 0), (U_c, 0), (W_i, 512), (U_i, 512), (W_c, 512), (U_c, 512)]
    weight_units = {("i", 0): (2, 3), ("c", 0): (4, 5), ("i", 1): (6, 7), ("c", 1): (8, 9)}

    with ExitStack() as ctx:
        const = ctx.enter_context(tc.tile_pool(name="const", bufs=1))
        rawp = ctx.enter_context(tc.tile_pool(name="rawp", bufs=1))
        keep = ctx.enter_context(tc.tile_pool(name="keep", bufs=1))
        grpp = ctx.enter_context(tc.tile_pool(name="grpp", bufs=6))
        work = ctx.enter_context(tc.tile_pool(name="work", bufs=3))
        sigp = ctx.enter_context(tc.tile_pool(name="sigp", bufs=6))
        rop = ctx.enter_context(tc.tile_pool(name="rop", bufs=1))
        psum = ctx.enter_context(tc.psum_pool(name="psum", bufs=8))
        ctx.enter_context(tc.manual_schedule())

        brow = const.tile([P, 2048], BF16, name="brow")
        ones = const.tile([P, P], BF16, name="ones")
        zeros = const.tile([P, 1], F32, name="zeros")
        warm = const.tile([P, 1], F32, name="warm")
        ident = const.tile([P, P], F32, name="ident")
        bias = const.tile([P, 2048], F32, name="bias")
        stat = const.tile([P, 12], F32, name="stat")
        pm = const.tile([P, 1], F32, name="pm")
        qs = const.tile([P, 4], F32, name="qs")
        rq = const.tile([P, 4], F32, name="rq")
        nc.vector.memset(zeros[:], 0.0)
        nc.vector.memset(brow[:], 0.0)
        nc.vector.memset(ones[:], 1.0)
        make_identity(nc, ident[:])
        nc.scalar.dma_start(out=brow[0:1, 0:1024], in_=b_W_i.rearrange("(o n) -> o n", o=1))
        nc.scalar.dma_start(out=brow[1:2, 0:1024], in_=b_U_i.rearrange("(o n) -> o n", o=1))
        nc.scalar.dma_start(out=brow[0:1, 1024:2048], in_=b_W_c.rearrange("(o n) -> o n", o=1))
        nc.scalar.dma_start(out=brow[1:2, 1024:2048], in_=b_U_c.rearrange("(o n) -> o n", o=1))
        nc.scalar.activation(out=warm[:], in_=zeros[:], func=ACT.Sigmoid)

        raw = {}
        for u in range(10):
            src, r0 = units[u]
            for pair in range(2):
                rows_in = src[r0 + pair * 256 : r0 + (pair + 1) * 256, :].rearrange("(p j) k -> p j k", j=2)
                if u == 0 and pair == 0:
                    for g in range(2):
                        t = rawp.tile([P, 2, 512], BF16, name="rawfirst%d" % g)
                        nc.sync.dma_start(out=t[:], in_=rows_in[:, :, g * 512 : (g + 1) * 512])
                        raw[4 * u + 2 * pair + g] = (t, 0)
                else:
                    t = rawp.tile([P, 2, 1024], BF16, name="raw%d_%d" % (u, pair))
                    nc.sync.dma_start(out=t[:], in_=rows_in)
                    for g in range(2):
                        raw[4 * u + 2 * pair + g] = (t, 256 * g)

        codes = {}
        scales = {}
        for u in range(10):
            for g in range(2):
                codes[(u, g)] = keep.tile([P, 512], U32, name="codes%d_%d" % (u, g), align_bytes=64)
                scales[(u, g)] = keep.tile([P, 512], U8, name="scales%d_%d" % (u, g), align_bytes=64)
        res = [keep.tile([P, 1024], F32, name="res%d" % m) for m in range(4)]
        res8 = [keep.tile([P, 1024], FP8, name="resb%d" % m) for m in range(4)]

        tps = {}
        grps = {}
        accs = {}
        sigs = {}
        cands = {}
        pending = []
        later = []
        head = [0]

        def transposes(b):
            words = raw[b][0][:].bitcast(F32)
            w0 = raw[b][1]
            tp = psum.tile([P, 512], F32, name="bank")
            for j in range(2):
                for e in range(2):
                    nc.tensor.transpose(tp[:, (2 * j + e) * P : (2 * j + e + 1) * P], words[:, j, w0 + e : w0 + 256 : 2], ident[:])
            tps[b] = tp

        def copy_out(b):
            grp = grpp.tile([P, 1024], BF16, name="grp", align_bytes=64)
            dst = grp[:].bitcast(F32).rearrange("p (j r e) -> p j r e", j=2, e=2)
            srcv = tps[b][:].rearrange("p (j e r) -> p j r e", j=2, e=2)
            if b < V_COPY_UNTIL and b % V_COPY_EVERY == V_COPY_EVERY - 1:
                nc.vector.tensor_copy(out=dst, in_=srcv)
            else:
                nc.scalar.copy(out=dst, in_=srcv)
            grps[b] = grp

        def quantize(b):
            u, pair, g = b // 4, (b % 4) // 2, b % 2
            cols = slice(pair * 256, (pair + 1) * 256)
            nc.vector.quantize_mx(out=codes[(u, g)][:, cols].bitcast(FP8X4), scales=scales[(u, g)][:, cols], in_=grps[b][:])

        def flush_quant():
            for b in pending:
                quantize(b)
            pending.clear()

        def pop_later(n_big):
            done = 0
            while head[0] < len(later) and done < n_big:
                big, fn = later[head[0]]
                head[0] += 1
                fn()
                if big:
                    done += 1

        def step_t(b):
            transposes(b)
            copy_out(b)
            flush_quant()
            pending.append(b)
            pop_later(1)

        def bias_rows():
            for q in range(4):
                bp = psum.tile([P, 512], F32, name="bank")
                nc.tensor.matmul(out=bp[:], lhsT=ones[:], rhs=brow[:, q * 512 : (q + 1) * 512], start=True, stop=True)
                nc.scalar.copy(out=bias[:, q * 512 : (q + 1) * 512], in_=bp[:])

        def group(gate, nh, m, c0=0, width=512):
            acc = psum.tile([P, width], F32, name="bank")
            rows = slice(m * P, (m + 1) * P)
            n = 0
            for a_unit, w_unit in zip((0, 1), weight_units[(gate, nh)]):
                for g in range(2):
                    nc.tensor.matmul_mx(
                        out=acc[:],
                        lhsT=codes[(a_unit, g)][:, rows].bitcast(FP8X4),
                        lhsT_scale=scales[(a_unit, g)][:, rows],
                        rhs=codes[(w_unit, g)][:, c0 : c0 + width].bitcast(FP8X4),
                        rhs_scale=scales[(w_unit, g)][:, c0 : c0 + width],
                        start=(n == 0),
                        stop=(n == 3),
                    )
                    n += 1
            return acc

        def add_bias(dst, acc_ap, bias_ap):
            nc.vector.tensor_tensor(
                out=dst.rearrange("p (b r j) -> p b r j", r=P, j=2),
                in0=acc_ap.rearrange("p (b j r) -> p b r j", r=P, j=2),
                in1=bias_ap.rearrange("p (b r j) -> p b r j", r=P, j=2),
                op=ALU.add,
            )

        def out_rows(m):
            return slice((m // 2) * 256 + m % 2, (m // 2 + 1) * 256, 2)

        def step_i(nh, m):
            flush_quant()
            acc = group("i", nh, m)
            pre = work.tile([P, 512], F32, name="pre")
            add_bias(pre[:], acc[:], bias[:, nh * 512 : (nh + 1) * 512])
            sig = sigp.tile([P, 512], F32, name="sig")
            nc.scalar.activation(out=sig[:], in_=pre[:], func=ACT.Sigmoid)
            sigs[(nh, m)] = sig
            pop_later(1)

        def store_bytes(m):
            nc.sync.dma_start(out=out_1[out_rows(m), :], in_=res8[m][:].bitcast(U8))

        def add_c(nh, m, c0=0, width=512):
            acc = group("c", nh, m, c0, width)
            if c0 == 0:
                cands[(nh, m)] = work.tile([P, 512], F32, name="cand")
            b0 = 1024 + nh * 512 + c0
            add_bias(cands[(nh, m)][:, c0 : c0 + width], acc[:], bias[:, b0 : b0 + width])

        def mult(eng, nh, m, c0=0, width=512):
            o0 = nh * 512 + c0
            eng.tensor_tensor(out=res[m][:, o0 : o0 + width], in0=sigs[(nh, m)][:, c0 : c0 + width], in1=cands[(nh, m)][:, c0 : c0 + width], op=ALU.mult)

        def store_half(nh, m):
            cols = slice(nh * 512, (nh + 1) * 512)
            nc.sync.dma_start(out=out_0[out_rows(m), cols], in_=res[m][:, cols])

        def amax(m, slot, o0, width):
            nc.vector.tensor_reduce(out=stat[:, 3 * m + slot : 3 * m + slot + 1], in_=res[m][:, o0 : o0 + width], axis=AX.X, op=ALU.max, apply_absolute_value=True)

        def qscale(m):
            nc.vector.tensor_scalar(out=qs[:, m : m + 1], in0=stat[:, 3 * m : 3 * m + 1], scalar1=stat[:, 3 * m + 1 : 3 * m + 2], scalar2=1.0 / 448.0, op0=ALU.max, op1=ALU.mult)

        def recip(m):
            nc.vector.reciprocal(out=rq[:, m : m + 1], in_=qs[:, m : m + 1])

        def cast_s(m, a, z):
            nc.scalar.activation(out=res8[m][:, a:z], in_=res[m][:, a:z], func=ACT.Identity, scale=rq[:, m : m + 1], bias=zeros[:, 0:1], saturate=False)

        def cast_v(m, a, z):
            nc.vector.tensor_scalar(out=res8[m][:, a:z], in0=res[m][:, a:z], scalar1=rq[:, m : m + 1], scalar2=None, op0=ALU.mult, saturate=False)

        ro = {}
        pres = {}

        def reorder(eng_is_vector, b):
            words = raw[b][0][:].bitcast(F32)
            w0 = raw[b][1]
            t = rop.tile([P, 512], F32, name="ro%d" % b)
            dst = t[:].rearrange("p (j e q) -> p j e q", j=2, e=2)
            srcv = words[:, :, w0 : w0 + 256].rearrange("p j (q e) -> p j e q", e=2)
            if eng_is_vector:
                nc.vector.tensor_copy(out=dst, in_=srcv)
            else:
                nc.scalar.copy(out=dst, in_=srcv)
            ro[b] = t

        def transposes_contig(b):
            tp = psum.tile([P, 512], F32, name="bank")
            for q in range(4):
                nc.tensor.transpose(tp[:, q * P : (q + 1) * P], ro[b][:, q * P : (q + 1) * P], ident[:])
            tps[b] = tp

        def gate_mm(nh, m):
            accs[("i", nh, m)] = group("i", nh, m)

        def gate_add(nh, m):
            pre = work.tile([P, 512], F32, name="pre")
            add_bias(pre[:], accs[("i", nh, m)][:], bias[:, nh * 512 : (nh + 1) * 512])
            pres[(nh, m)] = pre

        def gate_sig(nh, m):
            sig = sigp.tile([P, 512], F32, name="sig")
            nc.scalar.activation(out=sig[:], in_=pres[(nh, m)][:], func=ACT.Sigmoid)
            sigs[(nh, m)] = sig

        for b in range(32):
            transposes(b)
            copy_out(b)
            if b >= 1:
                quantize(b - 1)
            if b == 7:
                bias_rows()
        quantize(32 - 1)
        gate_mm(0, 0)
        reorder(False, 32)
        reorder(False, 33)
        reorder(False, 34)
        reorder(False, 35)
        gate_add(0, 0)
        gate_sig(0, 0)
        add_c(0, 0)
        mult(nc.gpsimd, 0, 0)
        store_half(0, 0)
        gate_mm(0, 1)
        reorder(False, 36)
        reorder(False, 37)
        gate_add(0, 1)
        gate_sig(0, 1)
        add_c(0, 1)
        mult(nc.gpsimd, 0, 1)
        store_half(0, 1)
        amax(0, 0, 0, 512)
        gate_mm(0, 2)
        reorder(False, 38)
        reorder(False, 39)
        gate_add(0, 2)
        add_c(0, 2)
        amax(1, 0, 0, 512)
        for b in range(32, 40):
            transposes_contig(b)
            copy_out(b)
            if b > 32:
                quantize(b - 1)
        quantize(39)
        gate_sig(0, 2)
        mult(nc.gpsimd, 0, 2)
        store_half(0, 2)
        gate_mm(0, 3)
        gate_add(0, 3)
        gate_sig(0, 3)
        add_c(0, 3)
        mult(nc.gpsimd, 0, 3)
        store_half(0, 3)
        gate_mm(1, 0)
        gate_mm(1, 1)
        gate_add(1, 0)
        gate_sig(1, 0)
        gate_add(1, 1)
        gate_sig(1, 1)
        add_c(1, 0)
        mult(nc.gpsimd, 1, 0)
        store_half(1, 0)
        amax(2, 0, 0, 512)
        add_c(1, 1)
        mult(nc.gpsimd, 1, 1)
        store_half(1, 1)
        amax(3, 0, 0, 512)
        gate_mm(1, 2)
        gate_add(1, 2)
        gate_sig(1, 2)
        amax(0, 1, 512, 512)
        add_c(1, 2)
        mult(nc.gpsimd, 1, 2)
        store_half(1, 2)
        qscale(0)
        amax(1, 1, 512, 512)
        recip(0)
        cast_s(0, 0, 1024)
        store_bytes(0)
        m = 3
        gate_mm(1, m)
        gate_add(1, m)
        gate_sig(1, m)
        qscale(1)
        add_c(1, m, 0, 256)
        recip(1)
        cast_s(1, 0, 1024)
        store_bytes(1)
        amax(2, 1, 512, 512)
        add_c(1, m, 256, 256)
        qscale(2)
        mult(nc.vector, 1, m, 0, 256)
        recip(2)
        mult(nc.vector, 1, m, 256, 256)
        cast_s(2, 0, 1024)
        store_bytes(2)
        store_half(1, m)
        amax(m, 1, 512, 256)
        amax(m, 2, 768, 256)
        nc.vector.tensor_scalar(out=pm[:], in0=stat[:, 3 * m : 3 * m + 1], scalar1=stat[:, 3 * m + 1 : 3 * m + 2], scalar2=1.0 / 448.0, op0=ALU.max, op1=ALU.mult)
        nc.vector.tensor_scalar(out=qs[:, m : m + 1], in0=stat[:, 3 * m + 2 : 3 * m + 3], scalar1=1.0 / 448.0, scalar2=pm[:, 0:1], op0=ALU.mult, op1=ALU.max)
        recip(m)
        cast_s(m, 0, S_CAST_COLS)
        cast_v(m, S_CAST_COLS, 1024)
        store_bytes(m)
